import numpy as np
import ml_dtypes


def mxq(x, axis, fmt="e4m3"):
    dtype, down = {"e4m3": (ml_dtypes.float8_e4m3fn, 7), "e5m2": (ml_dtypes.float8_e5m2, 14)}[fmt]
    v = np.moveaxis(np.asarray(x, np.float32).astype(ml_dtypes.bfloat16).astype(np.float64), axis, -1)
    blocks = v.reshape(v.shape[:-1] + (-1, 32))
    amax = np.abs(blocks).max(-1, keepdims=True)
    byte = np.maximum(np.where(amax > 0, np.frexp(amax)[1] - 1 + 127, 0) - down, 1)
    scale = np.exp2(byte - 127.0)
    codes = (blocks / scale).astype(np.float32).astype(dtype).astype(np.float64)
    return np.moveaxis((codes * scale).reshape(v.shape), -1, axis)


WIDE = False


def mx_kscale(k):
    if not WIDE:
        return np.ones(k)
    levels = np.array([10, -10, 5, -5, 0])
    if k % 512:
        return np.exp2(np.random.permutation(np.resize(levels, k // 32))).repeat(32)
    a = np.empty((k // 512, 16))
    for p in range(k // 512):
        a[p, :8] = np.random.permutation(np.resize(levels, 8))
        for g in range(8):
            far = levels[np.abs(levels - a[p, g]) >= 10]
            a[p, g + 8] = far[np.random.randint(len(far))]
    return np.exp2(a.ravel()).repeat(32)


BF16 = ml_dtypes.bfloat16


def bf(x):
    return np.asarray(x, np.float32).astype(BF16)


def f64(x):
    return np.asarray(x).astype(np.float64)


B, H, L, E, QD = 16, 1, 128, 2048, 128


def draw0():
    s = mx_kscale(E)
    return {"x": bf(np.random.standard_normal((B, H, L, E)) * s),
            "Wk": bf(np.random.standard_normal((QD, E)) * 0.3 / np.sqrt(E) / s),
            "bk": bf(0.1 + 0.1 * np.random.standard_normal(QD)),
            "Wv": bf(np.random.standard_normal((QD, E)) * 0.3 / np.sqrt(E) / s),
            "bv": bf(0.1 + 0.1 * np.random.standard_normal(QD))}


def core(x, Wk, bk, Wv, bv):
    xq = mxq(f64(x), 3, "e4m3")
    K = (xq @ mxq(f64(Wk), 1, "e4m3").T) + f64(bk)
    V = (xq @ mxq(f64(Wv), 1, "e4m3").T) + f64(bv)
    return K * V


def e4m3fn_bytes(y):
    return np.clip(np.asarray(y, np.float64), -448.0, 448.0).astype(np.float32).astype(ml_dtypes.float8_e4m3fn).view(np.uint8)


def e4m3fn_values(b):
    return np.asarray(b, np.uint8).view(ml_dtypes.float8_e4m3fn).astype(np.float64)


def setup_inputs():
    d = draw0()
    x0 = np.asarray(d['x']).astype(np.float64)
    s = (np.max(np.abs(x0), axis=(0, 1, 2), keepdims=True) / 448.0).astype(np.float32)
    out = {}
    for k, v in d.items():
        if k == 'x':
            out['x_bytes'] = e4m3fn_bytes(x0 / s.astype(np.float64))
            out['x_scale'] = s
        else:
            out[k] = v
    return out


def reference(x_bytes, x_scale, Wk, bk, Wv, bv):
    return core(e4m3fn_values(x_bytes) * x_scale.astype(np.float64), Wk, bk, Wv, bv)

@@ -1,0 +1,285 @@
+from contextlib import ExitStack
+
+import concourse.mybir as mybir
+from concourse.masks import make_identity
+
+F32 = mybir.dt.float32
+BF16 = mybir.dt.bfloat16
+U32 = mybir.dt.uint32
+U8 = mybir.dt.uint8
+FP8 = mybir.dt.float8_e4m3fn
+FP8X4 = mybir.dt.float8_e4m3fn_x4
+MULT = mybir.AluOpType.mult
+ADD = mybir.AluOpType.add
+IDENTITY = mybir.ActivationFunctionType.Identity
+COPY = mybir.ActivationFunctionType.Copy
+
+P = 128
+E = 2048
+ROWS = 2048
+QD = 128
+K_PASS = 512
+PASSES = E // K_PASS
+ROW_TILES = ROWS // P
+
+FLOPS = 2 * ROWS * E * 2 * QD
+
+B_ROWS = [0, 1]
+V_SETS = [[2, 3], [4, 5], [6, 7], [8, 9], [10, 11], [12, 13], [14], [15]]
+
+
+def tile_parallelretention_pa_kernel(tc, x_bytes, x_scale, Wk, bk, Wv, bv, out):
+    nc = tc.nc
+    x_rows = x_bytes.rearrange("b h l e -> (b h l) e")
+    out_tiles = out.rearrange("b h l q -> (b h l) q").rearrange("(n p) q -> p n q", p=P)
+    scale_row = x_scale.rearrange("a b c e -> (a b c e)")
+
+    with ExitStack() as ctx:
+        const = ctx.enter_context(tc.tile_pool(name="const", bufs=1))
+        xs_pool = ctx.enter_context(tc.tile_pool(name="xs", bufs=6))
+        g_pool = ctx.enter_context(tc.tile_pool(name="grouped", bufs=4))
+        q_pool = ctx.enter_context(tc.tile_pool(name="quant", bufs=3))
+        pl_pool = ctx.enter_context(tc.tile_pool(name="planes", bufs=2))
+        epi = ctx.enter_context(tc.tile_pool(name="epi", bufs=3))
+        tp_pool = ctx.enter_context(tc.psum_pool(name="tp", bufs=5))
+        acc_pool = ctx.enter_context(tc.psum_pool(name="acc", bufs=3))
+        ctx.enter_context(tc.manual_schedule())
+
+        xb = [const.tile([P, E], U8, name="xb%d" % r, tag="xb%d" % r) for r in range(ROW_TILES)]
+        sc = const.tile([P, E], F32, name="sc", tag="sc")
+        s16 = const.tile([P, PASSES, 4], F32, name="s16", tag="s16")
+        w_raw = [const.tile([P, E], BF16, name="wraw%d" % w, tag="wraw%d" % w) for w in range(2)]
+        bk_t = const.tile([P, 1], BF16, name="bk_t", tag="bk_t")
+        bv_t = const.tile([P, 1], BF16, name="bv_t", tag="bv_t")
+        b_row = const.tile([P, 2 * QD], BF16, name="b_row", tag="b_row")
+
+        def load_x(r):
+            nc.sync.dma_start(out=xb[r][:], in_=x_rows[r * P : (r + 1) * P, :])
+
+        def load_scale(c):
+            cols = slice(c * K_PASS, (c + 1) * K_PASS)
+            nc.sync.dma_start(out=sc[:, cols], in_=scale_row[cols].partition_broadcast(P))
+
+        load_scale(0)
+        for r in range(2, 6):
+            load_x(r)
+        load_scale(1)
+        load_scale(2)
+        load_scale(3)
+        load_x(0)
+        load_x(1)
+        load_x(6)
+        nc.sync.dma_start(out=w_raw[0][:], in_=Wk)
+        nc.sync.dma_start(out=w_raw[1][:], in_=Wv)
+        load_x(7)
+        nc.sync.dma_start(out=s16[:], in_=scale_row.rearrange("(g p t) -> p g t", g=PASSES, p=P, t=4))
+        load_x(8)
+        load_x(9)
+        nc.sync.dma_start(out=bk_t[:], in_=bk.rearrange("(p o) -> p o", o=1))
+        nc.sync.dma_start(out=bv_t[:], in_=bv.rearrange("(p o) -> p o", o=1))
+        for r in range(10, ROW_TILES):
+            load_x(r)
+        nc.sync.dma_start(out=b_row[:, 0:QD], in_=bk.partition_broadcast(P))
+        nc.sync.dma_start(out=b_row[:, QD : 2 * QD], in_=bv.partition_broadcast(P))
+
+        ident = const.tile([P, P], F32, name="ident", tag="ident")
+        make_identity(nc, ident[:])
+        warm_in = const.tile([P, 1], F32, name="warm_in", tag="warm_in")
+        warm_out = const.tile([P, 1], F32, name="warm_out", tag="warm_out")
+        nc.vector.memset(warm_in[:], 0.0)
+        nc.scalar.activation(out=warm_out[:], in_=warm_in[:], func=IDENTITY)
+
+        w_g = const.tile([P, PASSES * 2 * K_PASS], BF16, name="w_g", tag="w_g", align_bytes=64)
+        w_codes = const.tile([P, PASSES * 2 * P], U32, name="w_codes", tag="w_codes", align_bytes=64)
+        w_scl = const.tile([P, PASSES * 2 * P], U8, name="w_scl", tag="w_scl", align_bytes=64)
+
+        def widen(r, xs, c0, c1):
+            nc.vector.tensor_tensor(
+                out=xs[:, c0:c1], in0=xb[r][:, c0:c1].bitcast(FP8), in1=sc[:, c0:c1], op=MULT
+            )
+
+        def turn(src, grouped, n_r, r_in, g0, g1):
+            words = src[:].bitcast(F32)
+            gw = grouped[:].bitcast(F32).rearrange("p (g n r u) -> p g n r u", g=PASSES, n=n_r, r=P, u=2)
+            for b0 in range(g0, g1, 2):
+                b1 = min(b0 + 2, g1)
+                tp = tp_pool.tile([P, 2 * (b1 - b0), P], F32, name="tp", tag="tp")
+                for g in range(b0, b1):
+                    for u in range(2):
+                        nc.tensor.transpose(
+                            tp[:, 2 * (g - b0) + u, :], words[:, 256 * g + u : 256 * (g + 1) : 2], ident[:]
+                        )
+                nc.scalar.copy(
+                    out=gw[:, b0:b1, r_in, :, :], in_=tp[:].rearrange("p (g u) r -> p g r u", u=2)
+                )
+
+        def new_block(rows):
+            n_r = len(rows)
+            return {
+                "rows": rows,
+                "n_r": n_r,
+                "g": g_pool.tile([P, PASSES * n_r * K_PASS], BF16, name="grouped", tag="grouped", align_bytes=64),
+            }
+
+        def quantize_block(blk):
+            n_r = blk["n_r"]
+            blk["codes"] = q_pool.tile([P, PASSES * n_r * P], U32, name="codes", tag="codes", align_bytes=64)
+            blk["scl"] = q_pool.tile([P, PASSES * n_r * P], U8, name="scl", tag="scl", align_bytes=64)
+            nc.vector.quantize_mx(out=blk["codes"][:].bitcast(FP8X4), scales=blk["scl"][:], in_=blk["g"][:])
+
+        def project_block(blk):
+            n = blk["n_r"] * P
+            acc = acc_pool.tile([P, 512], F32, name="acc", tag="acc")
+            blk["k"] = acc[:, 0:n]
+            blk["v"] = acc[:, n : 2 * n]
+            for w, acc_ap in enumerate([blk["k"], blk["v"]]):
+                for g in range(PASSES):
+                    w_cols = slice((2 * g + w) * P, (2 * g + w + 1) * P)
+                    x_cols = slice(g * n, (g + 1) * n)
+                    nc.tensor.matmul_mx(
+                        out=acc_ap,
+                        lhsT=w_codes[:, w_cols].bitcast(FP8X4),
+                        lhsT_scale=w_scl[:, w_cols],
+                        rhs=blk["codes"][:, x_cols].bitcast(FP8X4),
+                        rhs_scale=blk["scl"][:, x_cols],
+                        start=(g == 0),
+                        stop=(g == PASSES - 1),
+                    )
+            ksb = epi.tile([P, 2 * P], F32, name="ksb", tag="ksb")
+            nc.scalar.activation(out=ksb[:, 0:n], in_=blk["k"], func=IDENTITY, bias=bk_t[:, 0:1], scale=1.0)
+            blk["ksb"] = ksb
+
+        def multiply(blk):
+            n = blk["n_r"] * P
+            kvt = epi.tile([P, 2 * P], F32, name="kvt", tag="kvt")
+            nc.vector.scalar_tensor_tensor(
+                out=kvt[:, 0:n], in0=blk["v"], scalar=bv_t[:, 0:1], in1=blk["ksb"][:, 0:n], op0=ADD, op1=MULT
+            )
+            blk["kvt"] = kvt
+
+        def turn_back(blk):
+            n_r = blk["n_r"]
+            kvt = blk["kvt"]
+            bt = tp_pool.tile([P, 2, P], F32, name="tp", tag="tp")
+            for i in range(n_r):
+                nc.tensor.transpose(bt[:, i, :], kvt[:, i * P : (i + 1) * P], ident[:])
+            osb = epi.tile([P, 2, P], F32, name="osb", tag="osb")
+            nc.scalar.copy(out=osb[:, 0:n_r, :], in_=bt[:, 0:n_r, :])
+            r0 = blk["rows"][0]
+            nc.sync.dma_start(out=out_tiles[:, r0 : r0 + n_r, :], in_=osb[:, 0:n_r, :])
+
+        def finish(blk):
+            multiply(blk)
+            turn_back(blk)
+
+        def project_rows(blk):
+            acc = acc_pool.tile([P, 512], F32, name="acc", tag="acc")
+            for g in range(PASSES):
+                nc.tensor.matmul_mx(
+                    out=acc[:, 0 : 2 * QD],
+                    lhsT=blk["codes"][:, g * P : (g + 1) * P].bitcast(FP8X4),
+                    lhsT_scale=blk["scl"][:, g * P : (g + 1) * P],
+                    rhs=w_codes[:, 2 * g * QD : 2 * (g + 1) * QD].bitcast(FP8X4),
+                    rhs_scale=w_scl[:, 2 * g * QD : 2 * (g + 1) * QD],
+                    start=(g == 0),
+                    stop=(g == PASSES - 1),
+                )
+            blk["kv"] = acc
+
+        def add_bias_rows(blk):
+            both = epi.tile([P, 2 * QD], F32, name="both", tag="both")
+            nc.vector.tensor_tensor(out=both[:], in0=blk["kv"][:, 0 : 2 * QD], in1=b_row[:], op=ADD)
+            blk["both"] = both
+
+        def multiply_rows(blk):
+            prod = epi.tile([P, QD], F32, name="prod", tag="prod")
+            nc.vector.tensor_tensor(out=prod[:], in0=blk["both"][:, 0:QD], in1=blk["both"][:, QD : 2 * QD], op=MULT)
+            nc.sync.dma_start(out=out_tiles[:, blk["rows"][0], :], in_=prod[:])
+
+        b_blk = {
+            "rows": B_ROWS,
+            "n_r": 2,
+            "g": const.tile([P, PASSES * 2 * K_PASS], BF16, name="b_g", tag="b_g", align_bytes=64),
+        }
+        b_cast_t = [const.tile([P, E], BF16, name="bcast%d" % i, tag="bcast%d" % i) for i in range(2)]
+        b_planes = {}
+
+        def b_cast(i):
+            nc.scalar.copy(out=b_cast_t[i][:], in_=xb[B_ROWS[i]][:].bitcast(FP8))
+
+        def b_turn(g):
+            tp = tp_pool.tile([P, 4, P], F32, name="tp", tag="tp")
+            for i in range(2):
+                words = b_cast_t[i][:].bitcast(F32)
+                for u in range(2):
+                    nc.tensor.transpose(tp[:, 2 * i + u, :], words[:, 256 * g + u : 256 * (g + 1) : 2], ident[:])
+            halves = tp[:].bitcast(BF16).rearrange("p (i u) (r e) -> p i u r e", u=2, e=2)
+            planes = pl_pool.tile([P, 4, 2, P], BF16, name="planes", tag="planes")
+            for t in range(4):
+                nc.scalar.activation(
+                    out=planes[:, t, :, :], in_=halves[:, :, t // 2, :, t % 2], func=COPY, scale=s16[:, g, t : t + 1]
+                )
+            b_planes[g] = planes
+
+        def b_weave(g):
+            woven = b_blk["g"][:].rearrange("p (g c t) -> p g c t", g=PASSES, t=4)
+            nc.scalar.copy(out=woven[:, g, :, :], in_=b_planes[g][:].rearrange("p t i r -> p (i r) t"))
+
+        def b_step(n):
+            if n < 2 * PASSES:
+                if n % 2 == 0:
+                    b_turn(n // 2)
+                else:
+                    b_weave(n // 2)
+
+        blocks = [new_block(V_SETS[0]), new_block(V_SETS[1])]
+
+        head_xs = [xs_pool.tile([P, E], BF16, name="xs", tag="xs", align_bytes=64) for r in range(4)]
+        for c0, c1 in [(0, 1), (1, 2)]:
+            for r in range(4):
+                widen(2 + r, head_xs[r], c0 * K_PASS, c1 * K_PASS)
+        for r in range(4):
+            turn(head_xs[r], blocks[r // 2]["g"], 2, r % 2, 0, 2)
+        b_cast(0)
+        turn(w_raw[0], w_g, 2, 0, 0, PASSES)
+        turn(w_raw[1], w_g, 2, 1, 0, PASSES)
+        for r in range(4):
+            widen(2 + r, head_xs[r], 2 * K_PASS, 4 * K_PASS)
+        for r in range(4):
+            turn(head_xs[r], blocks[r // 2]["g"], 2, r % 2, 2, 4)
+        b_cast(1)
+
+        window = 0
+        for i in range(5):
+            for rows in V_SETS[i + 2 : i + 3] if i < 4 else V_SETS[6:8]:
+                blk = new_block(rows)
+                blocks.append(blk)
+                for j, r in enumerate(rows):
+                    xs = xs_pool.tile([P, E], BF16, name="xs", tag="xs", align_bytes=64)
+                    widen(r, xs, 0, E)
+                    turn(xs, blk["g"], len(rows), j, 0, PASSES)
+                    b_step(window)
+                    window += 1
+            if i == 0:
+                nc.vector.quantize_mx(out=w_codes[:].bitcast(FP8X4), scales=w_scl[:], in_=w_g[:])
+            quantize_block(blocks[i])
+            project_block(blocks[i])
+            if i >= 1:
+                finish(blocks[i - 1])
+
+        quantize_block(b_blk)
+        project_block(b_blk)
+        quantize_block(blocks[5])
+        project_block(blocks[5])
+        finish(blocks[4])
+        quantize_block(blocks[6])
+        project_rows(blocks[6])
+        multiply(b_blk)
+        quantize_block(blocks[7])
+        project_rows(blocks[7])
+        turn_back(b_blk)
+        finish(blocks[5])
+        add_bias_rows(blocks[6])
+        add_bias_rows(blocks[7])
+        multiply_rows(blocks[6])
+        multiply_rows(blocks[7])

@@ -56,23 +56,17 @@ def tile_parallelretention_pa_kernel(tc, x_bytes, x_scale, Wk, bk, Wv, bv, out):
         def load_x(r):
             nc.sync.dma_start(out=xb[r][:], in_=x_rows[r * P : (r + 1) * P, :])
 
-        def load_scale(c):
-            cols = slice(c * K_PASS, (c + 1) * K_PASS)
-            nc.sync.dma_start(out=sc[:, cols], in_=scale_row[cols].partition_broadcast(P))
-
-        load_scale(0)
-        for r in range(2, 6):
+        nc.sync.dma_start(out=sc[:, 0:K_PASS], in_=scale_row[0:K_PASS].partition_broadcast(P))
+        load_x(2)
+        nc.sync.dma_start(out=s16[:], in_=scale_row.rearrange("(g p t) -> p g t", g=PASSES, p=P, t=4))
+        for r in range(3, 6):
             load_x(r)
-        load_scale(1)
-        load_scale(2)
-        load_scale(3)
         load_x(0)
         load_x(1)
         load_x(6)
         nc.sync.dma_start(out=w_raw[0][:], in_=Wk)
         nc.sync.dma_start(out=w_raw[1][:], in_=Wv)
         load_x(7)
-        nc.sync.dma_start(out=s16[:], in_=scale_row.rearrange("(g p t) -> p g t", g=PASSES, p=P, t=4))
         load_x(8)
         load_x(9)
         nc.sync.dma_start(out=bk_t[:], in_=bk.rearrange("(p o) -> p o", o=1))
@@ -92,6 +86,15 @@ def tile_parallelretention_pa_kernel(tc, x_bytes, x_scale, Wk, bk, Wv, bv, out):
         w_g = const.tile([P, PASSES * 2 * K_PASS], BF16, name="w_g", tag="w_g", align_bytes=64)
         w_codes = const.tile([P, PASSES * 2 * P], U32, name="w_codes", tag="w_codes", align_bytes=64)
         w_scl = const.tile([P, PASSES * 2 * P], U8, name="w_scl", tag="w_scl", align_bytes=64)
+
+        for g in range(1, PASSES):
+            spread = tp_pool.tile([P, 4, P], F32, name="tp", tag="tp")
+            for t in range(4):
+                nc.tensor.transpose(spread[:, t, :], s16[:, g, t : t + 1].to_broadcast([P, P]), ident[:])
+            nc.scalar.copy(
+                out=sc[:, g * K_PASS : (g + 1) * K_PASS].rearrange("p (n t) -> p n t", t=4),
+                in_=spread[:].rearrange("p t n -> p n t"),
+            )
 
         def widen(r, xs, c0, c1):
             nc.vector.tensor_tensor(

@@ -51,7 +51,8 @@ def tile_parallelretention_pa_kernel(tc, x_bytes, x_scale, Wk, bk, Wv, bv, out):
         w_raw = [const.tile([P, E], BF16, name="wraw%d" % w, tag="wraw%d" % w) for w in range(2)]
         bk_t = const.tile([P, 1], BF16, name="bk_t", tag="bk_t")
         bv_t = const.tile([P, 1], BF16, name="bv_t", tag="bv_t")
-        b_row = const.tile([P, 2 * QD], BF16, name="b_row", tag="b_row")
+        b_row2 = const.tile([P, 4 * QD], BF16, name="b_row2", tag="b_row2")
+        b_row = b_row2[:, 0 : 2 * QD]
 
         def load_x(r):
             nc.sync.dma_start(out=xb[r][:], in_=x_rows[r * P : (r + 1) * P, :])
@@ -73,8 +74,8 @@ def tile_parallelretention_pa_kernel(tc, x_bytes, x_scale, Wk, bk, Wv, bv, out):
         nc.sync.dma_start(out=bv_t[:], in_=bv.rearrange("(p o) -> p o", o=1))
         for r in range(10, ROW_TILES):
             load_x(r)
-        nc.sync.dma_start(out=b_row[:, 0:QD], in_=bk.partition_broadcast(P))
-        nc.sync.dma_start(out=b_row[:, QD : 2 * QD], in_=bv.partition_broadcast(P))
+        nc.sync.dma_start(out=b_row2[:, 0:QD], in_=bk.partition_broadcast(P))
+        nc.sync.dma_start(out=b_row2[:, QD : 2 * QD], in_=bv.partition_broadcast(P))
 
         ident = const.tile([P, P], F32, name="ident", tag="ident")
         make_identity(nc, ident[:])
@@ -191,7 +192,7 @@ def tile_parallelretention_pa_kernel(tc, x_bytes, x_scale, Wk, bk, Wv, bv, out):
 
         def add_bias_rows(blk):
             both = epi.tile([P, 2 * QD], F32, name="both", tag="both")
-            nc.vector.tensor_tensor(out=both[:], in0=blk["kv"][:, 0 : 2 * QD], in1=b_row[:], op=ADD)
+            nc.vector.tensor_tensor(out=both[:], in0=blk["kv"][:, 0 : 2 * QD], in1=b_row, op=ADD)
             blk["both"] = both
 
         def multiply_rows(blk):
@@ -253,16 +254,15 @@ def tile_parallelretention_pa_kernel(tc, x_bytes, x_scale, Wk, bk, Wv, bv, out):
         b_cast(1)
 
         window = 0
-        for i in range(5):
-            for rows in V_SETS[i + 2 : i + 3] if i < 4 else V_SETS[6:8]:
-                blk = new_block(rows)
-                blocks.append(blk)
-                for j, r in enumerate(rows):
-                    xs = xs_pool.tile([P, E], BF16, name="xs", tag="xs", align_bytes=64)
-                    widen(r, xs, 0, E)
-                    turn(xs, blk["g"], len(rows), j, 0, PASSES)
-                    b_step(window)
-                    window += 1
+        for i in range(4):
+            blk = new_block(V_SETS[i + 2])
+            blocks.append(blk)
+            for j, r in enumerate(V_SETS[i + 2]):
+                xs = xs_pool.tile([P, E], BF16, name="xs", tag="xs", align_bytes=64)
+                widen(r, xs, 0, E)
+                turn(xs, blk["g"], 2, j, 0, PASSES)
+                b_step(window)
+                window += 1
             if i == 0:
                 nc.vector.quantize_mx(out=w_codes[:].bitcast(FP8X4), scales=w_scl[:], in_=w_g[:])
             quantize_block(blocks[i])
@@ -270,19 +270,88 @@ def tile_parallelretention_pa_kernel(tc, x_bytes, x_scale, Wk, bk, Wv, bv, out):
             if i >= 1:
                 finish(blocks[i - 1])
 
-        quantize_block(b_blk)
-        project_block(b_blk)
+        def start_single(r):
+            blk = new_block([r])
+            blocks.append(blk)
+            blk["xs"] = xs_pool.tile([P, E], BF16, name="xs", tag="xs", align_bytes=64)
+            return blk
+
+        def widen_part(blk, g0, g1):
+            widen(blk["rows"][0], blk["xs"], g0 * K_PASS, g1 * K_PASS)
+            turn(blk["xs"], blk["g"], 1, 0, g0, g1)
+
+        def quantize_part(blk, g0, g1):
+            if g0 == 0:
+                blk["codes"] = q_pool.tile([P, PASSES * P], U32, name="codes", tag="codes", align_bytes=64)
+                blk["scl"] = q_pool.tile([P, PASSES * P], U8, name="scl", tag="scl", align_bytes=64)
+            nc.vector.quantize_mx(
+                out=blk["codes"][:, g0 * P : g1 * P].bitcast(FP8X4),
+                scales=blk["scl"][:, g0 * P : g1 * P],
+                in_=blk["g"][:, g0 * K_PASS : g1 * K_PASS],
+            )
+
+        def project_rows_part(blk, g0, g1):
+            if g0 == 0:
+                blk["kv"] = acc_pool.tile([P, 512], F32, name="acc", tag="acc")
+            for g in range(g0, g1):
+                nc.tensor.matmul_mx(
+                    out=blk["kv"][:, 0 : 2 * QD],
+                    lhsT=blk["codes"][:, g * P : (g + 1) * P].bitcast(FP8X4),
+                    lhsT_scale=blk["scl"][:, g * P : (g + 1) * P],
+                    rhs=w_codes[:, 2 * g * QD : 2 * (g + 1) * QD].bitcast(FP8X4),
+                    rhs_scale=w_scl[:, 2 * g * QD : 2 * (g + 1) * QD],
+                    start=(g == 0),
+                    stop=(g == PASSES - 1),
+                )
+
+
+        def project_rows_pair(blk):
+            acc = acc_pool.tile([P, 512], F32, name="acc", tag="acc")
+            for i in range(2):
+                for g in range(PASSES):
+                    nc.tensor.matmul_mx(
+                        out=acc[:, i * 2 * QD : (i + 1) * 2 * QD],
+                        lhsT=blk["codes"][:, (2 * g + i) * P : (2 * g + i + 1) * P].bitcast(FP8X4),
+                        lhsT_scale=blk["scl"][:, (2 * g + i) * P : (2 * g + i + 1) * P],
+                        rhs=w_codes[:, 2 * g * QD : 2 * (g + 1) * QD].bitcast(FP8X4),
+                        rhs_scale=w_scl[:, 2 * g * QD : 2 * (g + 1) * QD],
+                        start=(g == 0),
+                        stop=(g == PASSES - 1),
+                    )
+            blk["kv"] = acc
+
+        def add_bias_pair(blk):
+            both = epi.tile([P, 2, 2 * QD], F32, name="both2", tag="both2")
+            nc.vector.tensor_tensor(out=both[:].rearrange("p i q -> p (i q)"), in0=blk["kv"][:], in1=b_row2[:], op=ADD)
+            blk["both"] = both
+
+        def multiply_pair(blk):
+            prod = epi.tile([P, 2, QD], F32, name="prod2", tag="prod2")
+            nc.vector.tensor_tensor(out=prod[:], in0=blk["both"][:, :, 0:QD], in1=blk["both"][:, :, QD : 2 * QD], op=MULT)
+            r0 = blk["rows"][0]
+            nc.sync.dma_start(out=out_tiles[:, r0 : r0 + 2, :], in_=prod[:])
+
+        nc.scalar.copy(out=b_row2[:, 2 * QD : 4 * QD], in_=b_row2[:, 0 : 2 * QD])
+        quantize_block(blocks[4])
+        project_block(blocks[4])
+        t14 = start_single(14)
+        widen_part(t14, 0, 4)
+        finish(blocks[3])
         quantize_block(blocks[5])
         project_block(blocks[5])
+        t15 = start_single(15)
+        widen_part(t15, 0, 4)
         finish(blocks[4])
-        quantize_block(blocks[6])
-        project_rows(blocks[6])
-        multiply(b_blk)
-        quantize_block(blocks[7])
-        project_rows(blocks[7])
-        turn_back(b_blk)
+        quantize_block(b_blk)
+        project_rows_pair(b_blk)
+        quantize_part(t14, 0, 4)
+        project_rows_part(t14, 0, 4)
         finish(blocks[5])
-        add_bias_rows(blocks[6])
-        add_bias_rows(blocks[7])
-        multiply_rows(blocks[6])
-        multiply_rows(blocks[7])
+        quantize_part(t15, 0, 4)
+        project_rows_part(t15, 0, 4)
+        add_bias_pair(b_blk)
+        add_bias_rows(t14)
+        multiply_pair(b_blk)
+        multiply_rows(t14)
+        add_bias_rows(t15)
+        multiply_rows(t15)

@@ -59,7 +59,7 @@ def tile_parallelretention_pa_kernel(tc, x_bytes, x_scale, Wk, bk, Wv, bv, out):
 
         nc.sync.dma_start(out=sc[:, 0:K_PASS], in_=scale_row[0:K_PASS].partition_broadcast(P))
         load_x(2)
-        nc.sync.dma_start(out=s16[:], in_=scale_row.rearrange("(g p t) -> p g t", g=PASSES, p=P, t=4))
+        nc.scalar.dma_start(out=s16[:], in_=scale_row.rearrange("(g p t) -> p g t", g=PASSES, p=P, t=4))
         for r in range(3, 6):
             load_x(r)
         load_x(0)

@@ -57,10 +57,11 @@ def tile_parallelretention_pa_kernel(tc, x_bytes, x_scale, Wk, bk, Wv, bv, out):
         def load_x(r):
             nc.sync.dma_start(out=xb[r][:], in_=x_rows[r * P : (r + 1) * P, :])
 
-        nc.sync.dma_start(out=sc[:, 0:K_PASS], in_=scale_row[0:K_PASS].partition_broadcast(P))
-        load_x(2)
-        nc.scalar.dma_start(out=s16[:], in_=scale_row.rearrange("(g p t) -> p g t", g=PASSES, p=P, t=4))
-        for r in range(3, 6):
+        s16_src = scale_row.rearrange("(g p t) -> p g t", g=PASSES, p=P, t=4)
+        s4 = const.tile([P, 4], F32, name="s4", tag="s4")
+        nc.sync.dma_start(out=s4[:], in_=s16_src[:, 0, :])
+        nc.scalar.dma_start(out=s16[:], in_=s16_src)
+        for r in range(2, 6):
             load_x(r)
         load_x(0)
         load_x(1)
@@ -88,14 +89,16 @@ def tile_parallelretention_pa_kernel(tc, x_bytes, x_scale, Wk, bk, Wv, bv, out):
         w_codes = const.tile([P, PASSES * 2 * P], U32, name="w_codes", tag="w_codes", align_bytes=64)
         w_scl = const.tile([P, PASSES * 2 * P], U8, name="w_scl", tag="w_scl", align_bytes=64)
 
-        for g in range(1, PASSES):
+        for g in range(PASSES):
             spread = tp_pool.tile([P, 4, P], F32, name="tp", tag="tp")
             for t in range(4):
-                nc.tensor.transpose(spread[:, t, :], s16[:, g, t : t + 1].to_broadcast([P, P]), ident[:])
-            nc.scalar.copy(
-                out=sc[:, g * K_PASS : (g + 1) * K_PASS].rearrange("p (n t) -> p n t", t=4),
-                in_=spread[:].rearrange("p t n -> p n t"),
-            )
+                col = s4[:, t : t + 1] if g == 0 else s16[:, g, t : t + 1]
+                nc.tensor.transpose(spread[:, t, :], col.to_broadcast([P, P]), ident[:])
+            sc_out = sc[:, g * K_PASS : (g + 1) * K_PASS].rearrange("p (n t) -> p n t", t=4)
+            if g == 0:
+                nc.vector.tensor_copy(out=sc_out, in_=spread[:].rearrange("p t n -> p n t"))
+            else:
+                nc.scalar.copy(out=sc_out, in_=spread[:].rearrange("p t n -> p n t"))
 
         def widen(r, xs, c0, c1):
             nc.vector.tensor_tensor(

@@ -51,7 +51,8 @@ def tile_parallelretention_pa_kernel(tc, x_bytes, x_scale, Wk, bk, Wv, bv, out):
         w_raw = [const.tile([P, E], BF16, name="wraw%d" % w, tag="wraw%d" % w) for w in range(2)]
         bk_t = const.tile([P, 1], BF16, name="bk_t", tag="bk_t")
         bv_t = const.tile([P, 1], BF16, name="bv_t", tag="bv_t")
-        b_row2 = const.tile([P, 4 * QD], BF16, name="b_row2", tag="b_row2")
+        b_row2 = const.tile([P, 4 * QD], F32, name="b_row2", tag="b_row2")
+        b_col = const.tile([P, 2], F32, name="b_col", tag="b_col")
         b_row = b_row2[:, 0 : 2 * QD]
 
         def load_x(r):
@@ -61,6 +62,8 @@ def tile_parallelretention_pa_kernel(tc, x_bytes, x_scale, Wk, bk, Wv, bv, out):
         s4 = const.tile([P, 4], F32, name="s4", tag="s4")
         nc.sync.dma_start(out=s4[:], in_=s16_src[:, 0, :])
         nc.scalar.dma_start(out=s16[:], in_=s16_src)
+        nc.scalar.dma_start(out=bk_t[:], in_=bk.rearrange("(p o) -> p o", o=1))
+        nc.scalar.dma_start(out=bv_t[:], in_=bv.rearrange("(p o) -> p o", o=1))
         for r in range(2, 6):
             load_x(r)
         load_x(0)
@@ -71,12 +74,8 @@ def tile_parallelretention_pa_kernel(tc, x_bytes, x_scale, Wk, bk, Wv, bv, out):
         load_x(7)
         load_x(8)
         load_x(9)
-        nc.sync.dma_start(out=bk_t[:], in_=bk.rearrange("(p o) -> p o", o=1))
-        nc.sync.dma_start(out=bv_t[:], in_=bv.rearrange("(p o) -> p o", o=1))
         for r in range(10, ROW_TILES):
             load_x(r)
-        nc.sync.dma_start(out=b_row2[:, 0:QD], in_=bk.partition_broadcast(P))
-        nc.sync.dma_start(out=b_row2[:, QD : 2 * QD], in_=bv.partition_broadcast(P))
 
         ident = const.tile([P, P], F32, name="ident", tag="ident")
         make_identity(nc, ident[:])
@@ -99,6 +98,13 @@ def tile_parallelretention_pa_kernel(tc, x_bytes, x_scale, Wk, bk, Wv, bv, out):
                 nc.vector.tensor_copy(out=sc_out, in_=spread[:].rearrange("p t n -> p n t"))
             else:
                 nc.scalar.copy(out=sc_out, in_=spread[:].rearrange("p t n -> p n t"))
+
+        nc.scalar.copy(out=b_col[:, 0:1], in_=bk_t[:])
+        nc.scalar.copy(out=b_col[:, 1:2], in_=bv_t[:])
+        spread = tp_pool.tile([P, 4, P], F32, name="tp", tag="tp")
+        for j in range(4):
+            nc.tensor.transpose(spread[:, j, :], b_col[:, j % 2 : j % 2 + 1].to_broadcast([P, P]), ident[:])
+        nc.scalar.copy(out=b_row2[:], in_=spread[:].rearrange("p j q -> p (j q)"))
 
         def widen(r, xs, c0, c1):
             nc.vector.tensor_tensor(
@@ -334,7 +340,6 @@ def tile_parallelretention_pa_kernel(tc, x_bytes, x_scale, Wk, bk, Wv, bv, out):
             r0 = blk["rows"][0]
             nc.sync.dma_start(out=out_tiles[:, r0 : r0 + 2, :], in_=prod[:])
 
-        nc.scalar.copy(out=b_row2[:, 2 * QD : 4 * QD], in_=b_row2[:, 0 : 2 * QD])
         quantize_block(blocks[4])
         project_block(blocks[4])
         t14 = start_single(14)

@@ -185,28 +185,14 @@ def tile_parallelretention_pa_kernel(tc, x_bytes, x_scale, Wk, bk, Wv, bv, out):
             multiply(blk)
             turn_back(blk)
 
-        def project_rows(blk):
-            acc = acc_pool.tile([P, 512], F32, name="acc", tag="acc")
-            for g in range(PASSES):
-                nc.tensor.matmul_mx(
-                    out=acc[:, 0 : 2 * QD],
-                    lhsT=blk["codes"][:, g * P : (g + 1) * P].bitcast(FP8X4),
-                    lhsT_scale=blk["scl"][:, g * P : (g + 1) * P],
-                    rhs=w_codes[:, 2 * g * QD : 2 * (g + 1) * QD].bitcast(FP8X4),
-                    rhs_scale=w_scl[:, 2 * g * QD : 2 * (g + 1) * QD],
-                    start=(g == 0),
-                    stop=(g == PASSES - 1),
-                )
-            blk["kv"] = acc
-
         def add_bias_rows(blk):
             both = epi.tile([P, 2 * QD], F32, name="both", tag="both")
             nc.vector.tensor_tensor(out=both[:], in0=blk["kv"][:, 0 : 2 * QD], in1=b_row, op=ADD)
             blk["both"] = both
 
-        def multiply_rows(blk):
+        def multiply_rows(blk, engine):
             prod = epi.tile([P, QD], F32, name="prod", tag="prod")
-            nc.vector.tensor_tensor(out=prod[:], in0=blk["both"][:, 0:QD], in1=blk["both"][:, QD : 2 * QD], op=MULT)
+            engine.tensor_tensor(out=prod[:], in0=blk["both"][:, 0:QD], in1=blk["both"][:, QD : 2 * QD], op=MULT)
             nc.sync.dma_start(out=out_tiles[:, blk["rows"][0], :], in_=prod[:])
 
         b_blk = {
@@ -334,9 +320,9 @@ def tile_parallelretention_pa_kernel(tc, x_bytes, x_scale, Wk, bk, Wv, bv, out):
             nc.vector.tensor_tensor(out=both[:].rearrange("p i q -> p (i q)"), in0=blk["kv"][:], in1=b_row2[:], op=ADD)
             blk["both"] = both
 
-        def multiply_pair(blk):
+        def multiply_pair(blk, engine):
             prod = epi.tile([P, 2, QD], F32, name="prod2", tag="prod2")
-            nc.vector.tensor_tensor(out=prod[:], in0=blk["both"][:, :, 0:QD], in1=blk["both"][:, :, QD : 2 * QD], op=MULT)
+            engine.tensor_tensor(out=prod[:], in0=blk["both"][:, :, 0:QD], in1=blk["both"][:, :, QD : 2 * QD], op=MULT)
             r0 = blk["rows"][0]
             nc.sync.dma_start(out=out_tiles[:, r0 : r0 + 2, :], in_=prod[:])
 
@@ -348,18 +334,19 @@ def tile_parallelretention_pa_kernel(tc, x_bytes, x_scale, Wk, bk, Wv, bv, out):
         quantize_block(blocks[5])
         project_block(blocks[5])
         t15 = start_single(15)
-        widen_part(t15, 0, 4)
-        finish(blocks[4])
+        widen_part(t15, 0, 2)
+        widen_part(t15, 2, 4)
         quantize_block(b_blk)
         project_rows_pair(b_blk)
+        finish(blocks[4])
+        finish(blocks[5])
         quantize_part(t14, 0, 4)
         project_rows_part(t14, 0, 4)
-        finish(blocks[5])
         quantize_part(t15, 0, 4)
         project_rows_part(t15, 0, 4)
         add_bias_pair(b_blk)
+        multiply_pair(b_blk, nc.gpsimd)
         add_bias_rows(t14)
-        multiply_pair(b_blk)
-        multiply_rows(t14)
+        multiply_rows(t14, nc.gpsimd)
         add_bias_rows(t15)
-        multiply_rows(t15)
+        multiply_rows(t15, nc.vector)

@@ -332,14 +332,15 @@ def tile_parallelretention_pa_kernel(tc, x_bytes, x_scale, Wk, bk, Wv, bv, out):
         widen_part(t14, 0, 4)
         finish(blocks[3])
         quantize_block(blocks[5])
-        project_block(blocks[5])
+        project_rows_pair(blocks[5])
         t15 = start_single(15)
         widen_part(t15, 0, 2)
         widen_part(t15, 2, 4)
+        finish(blocks[4])
         quantize_block(b_blk)
         project_rows_pair(b_blk)
-        finish(blocks[4])
-        finish(blocks[5])
+        add_bias_pair(blocks[5])
+        multiply_pair(blocks[5], nc.gpsimd)
         quantize_part(t14, 0, 4)
         project_rows_part(t14, 0, 4)
         quantize_part(t15, 0, 4)

from contextlib import ExitStack

import concourse.mybir as mybir
from concourse.masks import make_identity

F32 = mybir.dt.float32
BF16 = mybir.dt.bfloat16
U32 = mybir.dt.uint32
U8 = mybir.dt.uint8
FP8 = mybir.dt.float8_e4m3fn
FP8X4 = mybir.dt.float8_e4m3fn_x4
MULT = mybir.AluOpType.mult
ADD = mybir.AluOpType.add
IDENTITY = mybir.ActivationFunctionType.Identity
COPY = mybir.ActivationFunctionType.Copy

P = 128
E = 2048
ROWS = 2048
QD = 128
K_PASS = 512
PASSES = E // K_PASS
ROW_TILES = ROWS // P

FLOPS = 2 * ROWS * E * 2 * QD

B_ROWS = [0, 1]
V_SETS = [[2, 3], [4, 5], [6, 7], [8, 9], [10, 11], [12, 13], [14], [15]]


def tile_parallelretention_pa_kernel(tc, x_bytes, x_scale, Wk, bk, Wv, bv, out):
    nc = tc.nc
    x_rows = x_bytes.rearrange("b h l e -> (b h l) e")
    out_tiles = out.rearrange("b h l q -> (b h l) q").rearrange("(n p) q -> p n q", p=P)
    scale_row = x_scale.rearrange("a b c e -> (a b c e)")

    with ExitStack() as ctx:
        const = ctx.enter_context(tc.tile_pool(name="const", bufs=1))
        xs_pool = ctx.enter_context(tc.tile_pool(name="xs", bufs=6))
        g_pool = ctx.enter_context(tc.tile_pool(name="grouped", bufs=4))
        q_pool = ctx.enter_context(tc.tile_pool(name="quant", bufs=3))
        pl_pool = ctx.enter_context(tc.tile_pool(name="planes", bufs=2))
        epi = ctx.enter_context(tc.tile_pool(name="epi", bufs=3))
        tp_pool = ctx.enter_context(tc.psum_pool(name="tp", bufs=5))
        acc_pool = ctx.enter_context(tc.psum_pool(name="acc", bufs=3))
        ctx.enter_context(tc.manual_schedule())

        xb = [const.tile([P, E], U8, name="xb%d" % r, tag="xb%d" % r) for r in range(ROW_TILES)]
        sc = const.tile([P, E], F32, name="sc", tag="sc")
        s16 = const.tile([P, PASSES, 4], F32, name="s16", tag="s16")
        w_raw = [const.tile([P, E], BF16, name="wraw%d" % w, tag="wraw%d" % w) for w in range(2)]
        bk_t = const.tile([P, 1], BF16, name="bk_t", tag="bk_t")
        bv_t = const.tile([P, 1], BF16, name="bv_t", tag="bv_t")
        b_row2 = const.tile([P, 4 * QD], F32, name="b_row2", tag="b_row2")
        b_col = const.tile([P, 2], F32, name="b_col", tag="b_col")
        b_row = b_row2[:, 0 : 2 * QD]

        def load_x(r):
            nc.sync.dma_start(out=xb[r][:], in_=x_rows[r * P : (r + 1) * P, :])

        s16_src = scale_row.rearrange("(g p t) -> p g t", g=PASSES, p=P, t=4)
        s4 = const.tile([P, 4], F32, name="s4", tag="s4")
        nc.sync.dma_start(out=s4[:], in_=s16_src[:, 0, :])
        nc.scalar.dma_start(out=s16[:], in_=s16_src)
        nc.scalar.dma_start(out=bk_t[:], in_=bk.rearrange("(p o) -> p o", o=1))
        nc.scalar.dma_start(out=bv_t[:], in_=bv.rearrange("(p o) -> p o", o=1))
        for r in range(2, 6):
            load_x(r)
        load_x(0)
        load_x(1)
        load_x(6)
        nc.sync.dma_start(out=w_raw[0][:], in_=Wk)
        nc.sync.dma_start(out=w_raw[1][:], in_=Wv)
        load_x(7)
        load_x(8)
        load_x(9)
        for r in range(10, ROW_TILES):
            load_x(r)

        ident = const.tile([P, P], F32, name="ident", tag="ident")
        make_identity(nc, ident[:])
        warm_in = const.tile([P, 1], F32, name="warm_in", tag="warm_in")
        warm_out = const.tile([P, 1], F32, name="warm_out", tag="warm_out")
        nc.vector.memset(warm_in[:], 0.0)
        nc.scalar.activation(out=warm_out[:], in_=warm_in[:], func=IDENTITY)

        w_g = const.tile([P, PASSES * 2 * K_PASS], BF16, name="w_g", tag="w_g", align_bytes=64)
        w_codes = const.tile([P, PASSES * 2 * P], U32, name="w_codes", tag="w_codes", align_bytes=64)
        w_scl = const.tile([P, PASSES * 2 * P], U8, name="w_scl", tag="w_scl", align_bytes=64)

        for g in range(PASSES):
            spread = tp_pool.tile([P, 4, P], F32, name="tp", tag="tp")
            for t in range(4):
                col = s4[:, t : t + 1] if g == 0 else s16[:, g, t : t + 1]
                nc.tensor.transpose(spread[:, t, :], col.to_broadcast([P, P]), ident[:])
            sc_out = sc[:, g * K_PASS : (g + 1) * K_PASS].rearrange("p (n t) -> p n t", t=4)
            if g == 0:
                nc.vector.tensor_copy(out=sc_out, in_=spread[:].rearrange("p t n -> p n t"))
            else:
                nc.scalar.copy(out=sc_out, in_=spread[:].rearrange("p t n -> p n t"))

        nc.scalar.copy(out=b_col[:, 0:1], in_=bk_t[:])
        nc.scalar.copy(out=b_col[:, 1:2], in_=bv_t[:])
        spread = tp_pool.tile([P, 4, P], F32, name="tp", tag="tp")
        for j in range(4):
            nc.tensor.transpose(spread[:, j, :], b_col[:, j % 2 : j % 2 + 1].to_broadcast([P, P]), ident[:])
        nc.scalar.copy(out=b_row2[:], in_=spread[:].rearrange("p j q -> p (j q)"))

        def widen(r, xs, c0, c1):
            nc.vector.tensor_tensor(
                out=xs[:, c0:c1], in0=xb[r][:, c0:c1].bitcast(FP8), in1=sc[:, c0:c1], op=MULT
            )

        def turn(src, grouped, n_r, r_in, g0, g1):
            words = src[:].bitcast(F32)
            gw = grouped[:].bitcast(F32).rearrange("p (g n r u) -> p g n r u", g=PASSES, n=n_r, r=P, u=2)
            for b0 in range(g0, g1, 2):
                b1 = min(b0 + 2, g1)
                tp = tp_pool.tile([P, 2 * (b1 - b0), P], F32, name="tp", tag="tp")
                for g in range(b0, b1):
                    for u in range(2):
                        nc.tensor.transpose(
                            tp[:, 2 * (g - b0) + u, :], words[:, 256 * g + u : 256 * (g + 1) : 2], ident[:]
                        )
                nc.scalar.copy(
                    out=gw[:, b0:b1, r_in, :, :], in_=tp[:].rearrange("p (g u) r -> p g r u", u=2)
                )

        def new_block(rows):
            n_r = len(rows)
            return {
                "rows": rows,
                "n_r": n_r,
                "g": g_pool.tile([P, PASSES * n_r * K_PASS], BF16, name="grouped", tag="grouped", align_bytes=64),
            }

        def quantize_block(blk):
            n_r = blk["n_r"]
            blk["codes"] = q_pool.tile([P, PASSES * n_r * P], U32, name="codes", tag="codes", align_bytes=64)
            blk["scl"] = q_pool.tile([P, PASSES * n_r * P], U8, name="scl", tag="scl", align_bytes=64)
            nc.vector.quantize_mx(out=blk["codes"][:].bitcast(FP8X4), scales=blk["scl"][:], in_=blk["g"][:])

        def project_block(blk):
            n = blk["n_r"] * P
            acc = acc_pool.tile([P, 512], F32, name="acc", tag="acc")
            blk["k"] = acc[:, 0:n]
            blk["v"] = acc[:, n : 2 * n]
            for w, acc_ap in enumerate([blk["k"], blk["v"]]):
                for g in range(PASSES):
                    w_cols = slice((2 * g + w) * P, (2 * g + w + 1) * P)
                    x_cols = slice(g * n, (g + 1) * n)
                    nc.tensor.matmul_mx(
                        out=acc_ap,
                        lhsT=w_codes[:, w_cols].bitcast(FP8X4),
                        lhsT_scale=w_scl[:, w_cols],
                        rhs=blk["codes"][:, x_cols].bitcast(FP8X4),
                        rhs_scale=blk["scl"][:, x_cols],
                        start=(g == 0),
                        stop=(g == PASSES - 1),
                    )
            ksb = epi.tile([P, 2 * P], F32, name="ksb", tag="ksb")
            nc.scalar.activation(out=ksb[:, 0:n], in_=blk["k"], func=IDENTITY, bias=bk_t[:, 0:1], scale=1.0)
            blk["ksb"] = ksb

        def multiply(blk):
            n = blk["n_r"] * P
            kvt = epi.tile([P, 2 * P], F32, name="kvt", tag="kvt")
            nc.vector.scalar_tensor_tensor(
                out=kvt[:, 0:n], in0=blk["v"], scalar=bv_t[:, 0:1], in1=blk["ksb"][:, 0:n], op0=ADD, op1=MULT
            )
            blk["kvt"] = kvt

        def turn_back(blk):
            n_r = blk["n_r"]
            kvt = blk["kvt"]
            bt = tp_pool.tile([P, 2, P], F32, name="tp", tag="tp")
            for i in range(n_r):
                nc.tensor.transpose(bt[:, i, :], kvt[:, i * P : (i + 1) * P], ident[:])
            osb = epi.tile([P, 2, P], F32, name="osb", tag="osb")
            nc.scalar.copy(out=osb[:, 0:n_r, :], in_=bt[:, 0:n_r, :])
            r0 = blk["rows"][0]
            nc.sync.dma_start(out=out_tiles[:, r0 : r0 + n_r, :], in_=osb[:, 0:n_r, :])

        def finish(blk):
            multiply(blk)
            turn_back(blk)

        def add_bias_rows(blk):
            both = epi.tile([P, 2 * QD], F32, name="both", tag="both")
            nc.vector.tensor_tensor(out=both[:], in0=blk["kv"][:, 0 : 2 * QD], in1=b_row, op=ADD)
            blk["both"] = both

        def multiply_rows(blk, engine):
            prod = epi.tile([P, QD], F32, name="prod", tag="prod")
            engine.tensor_tensor(out=prod[:], in0=blk["both"][:, 0:QD], in1=blk["both"][:, QD : 2 * QD], op=MULT)
            nc.sync.dma_start(out=out_tiles[:, blk["rows"][0], :], in_=prod[:])

        b_blk = {
            "rows": B_ROWS,
            "n_r": 2,
            "g": const.tile([P, PASSES * 2 * K_PASS], BF16, name="b_g", tag="b_g", align_bytes=64),
        }
        b_cast_t = [const.tile([P, E], BF16, name="bcast%d" % i, tag="bcast%d" % i) for i in range(2)]
        b_planes = {}

        def b_cast(i):
            nc.scalar.copy(out=b_cast_t[i][:], in_=xb[B_ROWS[i]][:].bitcast(FP8))

        def b_turn(g):
            tp = tp_pool.tile([P, 4, P], F32, name="tp", tag="tp")
            for i in range(2):
                words = b_cast_t[i][:].bitcast(F32)
                for u in range(2):
                    nc.tensor.transpose(tp[:, 2 * i + u, :], words[:, 256 * g + u : 256 * (g + 1) : 2], ident[:])
            halves = tp[:].bitcast(BF16).rearrange("p (i u) (r e) -> p i u r e", u=2, e=2)
            planes = pl_pool.tile([P, 4, 2, P], BF16, name="planes", tag="planes")
            for t in range(4):
                nc.scalar.activation(
                    out=planes[:, t, :, :], in_=halves[:, :, t // 2, :, t % 2], func=COPY, scale=s16[:, g, t : t + 1]
                )
            b_planes[g] = planes

        def b_weave(g):
            woven = b_blk["g"][:].rearrange("p (g c t) -> p g c t", g=PASSES, t=4)
            nc.scalar.copy(out=woven[:, g, :, :], in_=b_planes[g][:].rearrange("p t i r -> p (i r) t"))

        def b_step(n):
            if n < 2 * PASSES:
                if n % 2 == 0:
                    b_turn(n // 2)
                else:
                    b_weave(n // 2)

        blocks = [new_block(V_SETS[0]), new_block(V_SETS[1])]

        head_xs = [xs_pool.tile([P, E], BF16, name="xs", tag="xs", align_bytes=64) for r in range(4)]
        for c0, c1 in [(0, 1), (1, 2)]:
            for r in range(4):
                widen(2 + r, head_xs[r], c0 * K_PASS, c1 * K_PASS)
        for r in range(4):
            turn(head_xs[r], blocks[r // 2]["g"], 2, r % 2, 0, 2)
        b_cast(0)
        turn(w_raw[0], w_g, 2, 0, 0, PASSES)
        turn(w_raw[1], w_g, 2, 1, 0, PASSES)
        for r in range(4):
            widen(2 + r, head_xs[r], 2 * K_PASS, 4 * K_PASS)
        for r in range(4):
            turn(head_xs[r], blocks[r // 2]["g"], 2, r % 2, 2, 4)
        b_cast(1)

        window = 0
        for i in range(4):
            blk = new_block(V_SETS[i + 2])
            blocks.append(blk)
            for j, r in enumerate(V_SETS[i + 2]):
                xs = xs_pool.tile([P, E], BF16, name="xs", tag="xs", align_bytes=64)
                widen(r, xs, 0, E)
                turn(xs, blk["g"], 2, j, 0, PASSES)
                b_step(window)
                window += 1
            if i == 0:
                nc.vector.quantize_mx(out=w_codes[:].bitcast(FP8X4), scales=w_scl[:], in_=w_g[:])
            quantize_block(blocks[i])
            project_block(blocks[i])
            if i >= 1:
                finish(blocks[i - 1])

        def start_single(r):
            blk = new_block([r])
            blocks.append(blk)
            blk["xs"] = xs_pool.tile([P, E], BF16, name="xs", tag="xs", align_bytes=64)
            return blk

        def widen_part(blk, g0, g1):
            widen(blk["rows"][0], blk["xs"], g0 * K_PASS, g1 * K_PASS)
            turn(blk["xs"], blk["g"], 1, 0, g0, g1)

        def quantize_part(blk, g0, g1):
            if g0 == 0:
                blk["codes"] = q_pool.tile([P, PASSES * P], U32, name="codes", tag="codes", align_bytes=64)
                blk["scl"] = q_pool.tile([P, PASSES * P], U8, name="scl", tag="scl", align_bytes=64)
            nc.vector.quantize_mx(
                out=blk["codes"][:, g0 * P : g1 * P].bitcast(FP8X4),
                scales=blk["scl"][:, g0 * P : g1 * P],
                in_=blk["g"][:, g0 * K_PASS : g1 * K_PASS],
            )

        def project_rows_part(blk, g0, g1):
            if g0 == 0:
                blk["kv"] = acc_pool.tile([P, 512], F32, name="acc", tag="acc")
            for g in range(g0, g1):
                nc.tensor.matmul_mx(
                    out=blk["kv"][:, 0 : 2 * QD],
                    lhsT=blk["codes"][:, g * P : (g + 1) * P].bitcast(FP8X4),
                    lhsT_scale=blk["scl"][:, g * P : (g + 1) * P],
                    rhs=w_codes[:, 2 * g * QD : 2 * (g + 1) * QD].bitcast(FP8X4),
                    rhs_scale=w_scl[:, 2 * g * QD : 2 * (g + 1) * QD],
                    start=(g == 0),
                    stop=(g == PASSES - 1),
                )


        def project_rows_pair(blk):
            acc = acc_pool.tile([P, 512], F32, name="acc", tag="acc")
            for i in range(2):
                for g in range(PASSES):
                    nc.tensor.matmul_mx(
                        out=acc[:, i * 2 * QD : (i + 1) * 2 * QD],
                        lhsT=blk["codes"][:, (2 * g + i) * P : (2 * g + i + 1) * P].bitcast(FP8X4),
                        lhsT_scale=blk["scl"][:, (2 * g + i) * P : (2 * g + i + 1) * P],
                        rhs=w_codes[:, 2 * g * QD : 2 * (g + 1) * QD].bitcast(FP8X4),
                        rhs_scale=w_scl[:, 2 * g * QD : 2 * (g + 1) * QD],
                        start=(g == 0),
                        stop=(g == PASSES - 1),
                    )
            blk["kv"] = acc

        def add_bias_pair(blk):
            both = epi.tile([P, 2, 2 * QD], F32, name="both2", tag="both2")
            nc.vector.tensor_tensor(out=both[:].rearrange("p i q -> p (i q)"), in0=blk["kv"][:], in1=b_row2[:], op=ADD)
            blk["both"] = both

        def multiply_pair(blk, engine):
            prod = epi.tile([P, 2, QD], F32, name="prod2", tag="prod2")
            engine.tensor_tensor(out=prod[:], in0=blk["both"][:, :, 0:QD], in1=blk["both"][:, :, QD : 2 * QD], op=MULT)
            r0 = blk["rows"][0]
            nc.sync.dma_start(out=out_tiles[:, r0 : r0 + 2, :], in_=prod[:])

        quantize_block(blocks[4])
        project_block(blocks[4])
        t14 = start_single(14)
        widen_part(t14, 0, 4)
        finish(blocks[3])
        quantize_block(blocks[5])
        project_rows_pair(blocks[5])
        t15 = start_single(15)
        widen_part(t15, 0, 2)
        widen_part(t15, 2, 4)
        finish(blocks[4])
        quantize_block(b_blk)
        project_rows_pair(b_blk)
        add_bias_pair(blocks[5])
        multiply_pair(blocks[5], nc.gpsimd)
        quantize_part(t14, 0, 4)
        project_rows_part(t14, 0, 4)
        quantize_part(t15, 0, 4)
        project_rows_part(t15, 0, 4)
        add_bias_pair(b_blk)
        multiply_pair(b_blk, nc.gpsimd)
        add_bias_rows(t14)
        multiply_rows(t14, nc.gpsimd)
        add_bias_rows(t15)
        multiply_rows(t15, nc.vector)
